import numpy as np
import ml_dtypes


def mxq(x, axis, fmt="e4m3"):
    dtype, down = {"e4m3": (ml_dtypes.float8_e4m3fn, 7), "e5m2": (ml_dtypes.float8_e5m2, 14)}[fmt]
    v = np.moveaxis(np.asarray(x, np.float32).astype(ml_dtypes.bfloat16).astype(np.float64), axis, -1)
    blocks = v.reshape(v.shape[:-1] + (-1, 32))
    amax = np.abs(blocks).max(-1, keepdims=True)
    byte = np.maximum(np.where(amax > 0, np.frexp(amax)[1] - 1 + 127, 0) - down, 1)
    scale = np.exp2(byte - 127.0)
    codes = (blocks / scale).astype(np.float32).astype(dtype).astype(np.float64)
    return np.moveaxis((codes * scale).reshape(v.shape), -1, axis)


WIDE = False


def mx_kscale(k):
    if not WIDE:
        return np.ones(k)
    levels = np.array([10, -10, 5, -5, 0])
    a = np.random.permutation(np.resize(levels, k // 512 * 4)).reshape(k // 512, 4)
    idx = np.arange(k)
    return np.exp2(a[idx // 512, idx % 128 // 32])


BF16 = ml_dtypes.bfloat16


def bf(x):
    return np.asarray(x, np.float32).astype(BF16)


def f64(x):
    return np.asarray(x).astype(np.float64)


B, E, P, H, HK, D = 4, 128, 384, 4, 2, 128
G = H // HK
S = P + E
SCALING = 1.0 / np.sqrt(D)


def setup_inputs():
    s = mx_kscale(S)
    a = np.log2(s)
    g = s.max() / s
    q = np.random.standard_normal((B, E, H, D)) * 2.0
    k = np.random.standard_normal((B, E, HK, D))
    v = np.random.standard_normal((B, E, HK, D)) * 2.0
    k_cache = np.random.standard_normal((B, P, HK, D))
    v_cache = np.random.standard_normal((B, P, HK, D)) * 2.0
    q[..., 0] = np.log(2.0) * np.sqrt(D)
    k_cache[..., 0] += a[:P][None, :, None]
    k[..., 0] += a[P:][None, :, None]
    v_cache *= g[:P][None, :, None, None]
    v *= g[P:][None, :, None, None]
    return {"q": bf(q), "k": bf(k), "v": bf(v), "k_cache": bf(k_cache), "v_cache": bf(v_cache)}


def reference(q, k, v, k_cache, v_cache):
    k_all = np.concatenate([f64(k_cache), f64(k)], axis=1)
    v_all = np.concatenate([f64(v_cache), f64(v)], axis=1)
    qg = f64(q).reshape(B, E, HK, G, D).transpose(0, 2, 3, 1, 4).reshape(B, HK, G * E, D)
    scores = ((qg @ k_all.transpose(0, 2, 3, 1)) * SCALING).reshape(B, HK, G, E, S)
    visible = np.arange(S)[None, :] <= (P + np.arange(E))[:, None]
    scores = np.where(visible[None, None, None, :, :], scores, -1e30)
    e = np.exp(scores - scores.max(-1, keepdims=True))
    o = mxq(e, 4, "e4m3").reshape(B, HK, G * E, S) @ mxq(v_all, 1, "e4m3").transpose(0, 2, 1, 3)
    o = o.reshape(B, HK, G, E, D) / e.sum(-1, keepdims=True)
    return o.transpose(0, 3, 1, 2, 4).reshape(B * E, H * D)

@@ -1,0 +1,319 @@
+import math
+from contextlib import ExitStack
+
+import concourse.mybir as mybir
+from concourse.masks import make_identity
+
+BF16 = mybir.dt.bfloat16
+F32 = mybir.dt.float32
+U32 = mybir.dt.uint32
+U8 = mybir.dt.uint8
+FP8X4 = mybir.dt.float8_e4m3fn_x4
+ALU = mybir.AluOpType
+ACT = mybir.ActivationFunctionType
+AX = mybir.AxisListType
+
+B = 4
+E = 128
+PREFIX = 384
+S = PREFIX + E
+H = 4
+HK = 2
+G = H // HK
+D = 128
+P = 128
+SCALING = 1.0 / math.sqrt(D)
+HIDDEN = -1.0e30
+
+FLOPS = 2 * 2 * B * H * E * S * D
+
+
+N_HEADS = B * H
+N_PAIRS = B * HK
+
+
+def sequence_that_starts_at(n):
+    return n // H if 0 <= n < N_HEADS and n % H == 0 else None
+
+
+def pair_that_ends_at(n):
+    return n // G if 0 <= n < N_HEADS and n % G == G - 1 else None
+
+
+def tile_radixattention_s_kernel(tc, q, k, v, k_cache, v_cache, out):
+    nc = tc.nc
+    with ExitStack() as ctx:
+        consts = ctx.enter_context(tc.tile_pool(name="consts", bufs=1))
+        keep = ctx.enter_context(tc.tile_pool(name="keep", bufs=1))
+        banks = ctx.enter_context(tc.psum_pool(name="banks", bufs=8))
+        ctx.enter_context(tc.manual_schedule())
+
+        ident_bf = consts.tile([P, P], BF16, name="ident_bf")
+        make_identity(nc, ident_bf[:])
+        causal = consts.tile([P, E], F32, name="causal")
+        nc.gpsimd.memset(causal[:], 0.0)
+        nc.gpsimd.affine_select(
+            out=causal[:],
+            in_=causal[:],
+            compare_op=ALU.is_ge,
+            fill=HIDDEN,
+            base=0,
+            pattern=[[-1, E]],
+            channel_multiplier=1,
+        )
+        ident_f32 = consts.tile([P, P], F32, name="ident_f32")
+        make_identity(nc, ident_f32[:])
+        warm_in = consts.tile([P, 1], F32, name="warm_in")
+        warm_out = consts.tile([P, 1], F32, name="warm_out")
+        nc.vector.memset(warm_in[:], 0.0)
+        nc.scalar.activation(out=warm_out[:], in_=warm_in[:], func=ACT.Exp)
+
+        q_rows, k_rows, v_rows = {}, {}, {}
+        qT_ps, kT_ps, qT, kT = {}, {}, {}, {}
+        v_grouped, v_codes, v_scales = {}, {}, {}
+        diag_ps, masked, diag_max, prefix_max, neg_max = {}, {}, {}, {}, {}
+        prefix_sum, diag_sum, row_sum, inv_sum = {}, {}, {}, {}
+        prefix_ps, e_rows = {}, {}
+        eT_ps, e_grouped, e_codes, e_scales, o_ps = {}, {}, {}, {}, {}
+
+        def load_qk(b):
+            q_rows[b] = keep.tile([P, H * D], BF16, name="q_rows%d" % b)
+            nc.sync.dma_start(out=q_rows[b][:], in_=q[b].rearrange("e h d -> e (h d)"))
+            k_rows[b] = keep.tile([P, S // P, HK * D], BF16, name="k_rows%d" % b)
+            nc.sync.dma_start(
+                out=k_rows[b][:, 0 : PREFIX // P, :],
+                in_=k_cache[b].rearrange("(t p) g d -> p t (g d)", p=P),
+            )
+            nc.sync.dma_start(
+                out=k_rows[b][:, PREFIX // P, :], in_=k[b].rearrange("e g d -> e (g d)")
+            )
+
+        def load_v(b):
+            v_rows[b] = keep.tile([P, 4, HK * D], BF16, name="v_rows%d" % b)
+            nc.sync.dma_start(
+                out=v_rows[b][:, 0:2, :].rearrange("p t c -> p (t c)"),
+                in_=v_cache[b, 0:256].rearrange("(p e) g d -> p (e g d)", e=2),
+            )
+            nc.sync.dma_start(
+                out=v_rows[b][0:64, 2:4, :].rearrange("p t c -> p (t c)"),
+                in_=v_cache[b, 256:PREFIX].rearrange("(p e) g d -> p (e g d)", e=2),
+            )
+            nc.sync.dma_start(
+                out=v_rows[b][64:P, 2:4, :].rearrange("p t c -> p (t c)"),
+                in_=v[b].rearrange("(p e) g d -> p (e g d)", e=2),
+            )
+
+        def transpose_qk(b):
+            qT_ps[b] = banks.tile([P, H * E], BF16, name="qT_ps", tag="bank")
+            for h in range(H):
+                cols = slice(h * D, (h + 1) * D)
+                nc.tensor.transpose(qT_ps[b][:, cols], q_rows[b][:, cols], ident_bf[:])
+            for g in range(HK):
+                kT_ps[b, g] = banks.tile([P, S], BF16, name="kT_ps", tag="bank")
+                for t in range(S // P):
+                    nc.tensor.transpose(
+                        kT_ps[b, g][:, t * P : (t + 1) * P],
+                        k_rows[b][:, t, g * D : (g + 1) * D],
+                        ident_bf[:],
+                    )
+
+        def copy_qk(b):
+            qT[b] = keep.tile([P, H * E], BF16, name="qT%d" % b)
+            kT[b] = keep.tile([P, HK, S], BF16, name="kT%d" % b)
+            nc.scalar.copy(out=qT[b][:], in_=qT_ps[b][:])
+            nc.vector.tensor_copy(out=kT[b][:, 0, :], in_=kT_ps[b, 0][:])
+            nc.scalar.copy(out=kT[b][:, 1, :], in_=kT_ps[b, 1][:])
+
+        def regroup_v(b):
+            v_grouped[b] = keep.tile(
+                [P, HK * D, 4], BF16, name="v_grouped%d" % b, align_bytes=64
+            )
+            nc.vector.tensor_copy(
+                out=v_grouped[b][:], in_=v_rows[b][:].rearrange("p t c -> p c t")
+            )
+
+        def quantise_v(b):
+            v_codes[b] = keep.tile([P, HK * D], U32, name="v_codes%d" % b, align_bytes=64)
+            v_scales[b] = keep.tile([P, HK * D], U8, name="v_scales%d" % b, align_bytes=64)
+            nc.vector.quantize_mx(
+                out=v_codes[b][:].bitcast(FP8X4),
+                scales=v_scales[b][:],
+                in_=v_grouped[b][:].rearrange("p c t -> p (c t)"),
+            )
+
+        def score_diag(b):
+            diag_ps[b] = banks.tile([P, H, E], F32, name="diag_ps", tag="bank")
+            for h in range(H):
+                nc.tensor.matmul(
+                    out=diag_ps[b][:, h, :],
+                    lhsT=qT[b][:, h * E : (h + 1) * E],
+                    rhs=kT[b][:, h // G, PREFIX:S],
+                    start=True,
+                    stop=True,
+                )
+
+        def mask_diag(b):
+            masked[b] = keep.tile([P, H, E], F32, name="masked%d" % b)
+            prefix_max[b] = keep.tile([P, H], F32, name="prefix_max%d" % b)
+            neg_max[b] = keep.tile([P, H], F32, name="neg_max%d" % b)
+            prefix_sum[b] = keep.tile([P, H], F32, name="prefix_sum%d" % b)
+            diag_sum[b] = keep.tile([P, H], F32, name="diag_sum%d" % b)
+            nc.vector.tensor_tensor(
+                out=masked[b][:],
+                in0=diag_ps[b][:],
+                in1=causal[:].unsqueeze(1).to_broadcast([P, H, E]),
+                op=ALU.add,
+            )
+
+        def max_diag(b):
+            diag_max[b] = keep.tile([P, H], F32, name="diag_max%d" % b)
+            nc.vector.tensor_reduce(out=diag_max[b][:], in_=masked[b][:], axis=AX.X, op=ALU.max)
+
+        def score_prefix(n):
+            b, h = divmod(n, H)
+            prefix_ps[n] = banks.tile([P, PREFIX], F32, name="prefix_ps", tag="bank")
+            nc.tensor.matmul(
+                out=prefix_ps[n][:],
+                lhsT=qT[b][:, h * E : (h + 1) * E],
+                rhs=kT[b][:, h // G, 0:PREFIX],
+                start=True,
+                stop=True,
+            )
+
+        def max_prefix(n):
+            b, h = divmod(n, H)
+            nc.vector.tensor_reduce(
+                out=prefix_max[b][:, h : h + 1], in_=prefix_ps[n][:], axis=AX.X, op=ALU.max
+            )
+
+        def exp_bias(n):
+            b, h = divmod(n, H)
+            nc.vector.tensor_scalar(
+                out=neg_max[b][:, h : h + 1],
+                in0=prefix_max[b][:, h : h + 1],
+                scalar1=diag_max[b][:, h : h + 1],
+                scalar2=-SCALING,
+                op0=ALU.max,
+                op1=ALU.mult,
+            )
+
+        def exponentials(n):
+            b, h = divmod(n, H)
+            e_rows[n] = keep.tile([P, S], BF16, name="e_rows%d" % n)
+            nc.scalar.activation(
+                out=e_rows[n][:, 0:PREFIX],
+                in_=prefix_ps[n][:],
+                func=ACT.Exp,
+                bias=neg_max[b][:, h : h + 1],
+                scale=SCALING,
+                accum_out=prefix_sum[b][:, h : h + 1],
+            )
+            nc.scalar.activation(
+                out=e_rows[n][:, PREFIX:S],
+                in_=masked[b][:, h, :],
+                func=ACT.Exp,
+                bias=neg_max[b][:, h : h + 1],
+                scale=SCALING,
+                accum_out=diag_sum[b][:, h : h + 1],
+            )
+
+        def transpose_e(p):
+            eT_ps[p] = banks.tile([P, G, 2, E], F32, name="eT_ps", tag="bank")
+            for a in range(G):
+                words = e_rows[p * G + a][:].bitcast(F32)
+                for u in range(2):
+                    nc.tensor.transpose(
+                        eT_ps[p][:, a, u, :], words[:, u * P : (u + 1) * P], ident_f32[:]
+                    )
+
+        def regroup_e(p):
+            e_grouped[p] = keep.tile(
+                [P, G * E * 4], BF16, name="e_grouped%d" % p, align_bytes=64
+            )
+            nc.scalar.copy(
+                out=e_grouped[p][:].bitcast(F32).rearrange("p (a i u) -> p a i u", a=G, u=2),
+                in_=eT_ps[p][:].rearrange("p a u i -> p a i u"),
+            )
+
+        def quantise_e(p):
+            e_codes[p] = keep.tile([P, G * E], U32, name="e_codes%d" % p, align_bytes=64)
+            e_scales[p] = keep.tile([P, G * E], U8, name="e_scales%d" % p, align_bytes=64)
+            nc.vector.quantize_mx(
+                out=e_codes[p][:].bitcast(FP8X4), scales=e_scales[p][:], in_=e_grouped[p][:]
+            )
+
+        def multiply_v(p):
+            b, g = divmod(p, HK)
+            if g == 0:
+                o_ps[b] = banks.tile([P, H, D], F32, name="o_ps", tag="bank")
+            for a in range(G):
+                nc.tensor.matmul_mx(
+                    out=o_ps[b][:, g * G + a, :],
+                    lhsT=e_codes[p][:, a * E : (a + 1) * E].bitcast(FP8X4),
+                    lhsT_scale=e_scales[p][:, a * E : (a + 1) * E],
+                    rhs=v_codes[b][:, g * D : (g + 1) * D].bitcast(FP8X4),
+                    rhs_scale=v_scales[b][:, g * D : (g + 1) * D],
+                    start=True,
+                    stop=True,
+                )
+
+        def sum_rows(b):
+            row_sum[b] = keep.tile([P, H], F32, name="row_sum%d" % b)
+            nc.vector.tensor_tensor(
+                out=row_sum[b][:], in0=prefix_sum[b][:], in1=diag_sum[b][:], op=ALU.add
+            )
+
+        def invert_sums(b):
+            inv_sum[b] = keep.tile([P, H], F32, name="inv_sum%d" % b)
+            nc.vector.reciprocal(out=inv_sum[b][:], in_=row_sum[b][:])
+
+        def normalise_and_store(p):
+            b, g = divmod(p, HK)
+            heads = slice(g * G, (g + 1) * G)
+            o_sb = keep.tile([P, G, D], F32, name="o_sb%d" % p)
+            nc.vector.tensor_tensor(
+                out=o_sb[:],
+                in0=o_ps[b][:, heads, :],
+                in1=inv_sum[b][:, heads].unsqueeze(2).to_broadcast([P, G, D]),
+                op=ALU.mult,
+            )
+            nc.sync.dma_start(
+                out=out[b * E : (b + 1) * E, g * G * D : (g + 1) * G * D],
+                in_=o_sb[:].rearrange("p a d -> p (a d)"),
+            )
+
+        def when(index, stage):
+            if index is not None:
+                stage(index)
+
+        def unit(n):
+            return n if 0 <= n < N_HEADS else None
+
+        load_qk(0)
+        for b in range(B):
+            if b + 1 < B:
+                load_qk(b + 1)
+            load_v(b)
+
+        for s in range(-5, N_HEADS + 3):
+            when(sequence_that_starts_at(s + 5), transpose_qk)
+            when(sequence_that_starts_at(s + 4), score_diag)
+            when(unit(s + 3), score_prefix)
+
+            when(sequence_that_starts_at(s - 4), sum_rows)
+            when(unit(s + 2), max_prefix)
+            when(pair_that_ends_at(s - 2), quantise_e)
+            when(sequence_that_starts_at(s + 2), max_diag)
+            when(sequence_that_starts_at(s - 4), invert_sums)
+            when(unit(s + 2), exp_bias)
+            when(pair_that_ends_at(s - 3), normalise_and_store)
+
+            when(pair_that_ends_at(s - 2), multiply_v)
+            when(unit(s), exponentials)
+            when(pair_that_ends_at(s), transpose_e)
+            when(pair_that_ends_at(s - 1), regroup_e)
+            when(sequence_that_starts_at(s + 5), copy_qk)
+
+            when(sequence_that_starts_at(s + 3), mask_diag)
+            when(sequence_that_starts_at(s), regroup_v)
+            when(sequence_that_starts_at(s - 2), quantise_v)

@@ -128,8 +128,13 @@ def tile_radixattention_s_kernel(tc, q, k, v, k_cache, v_cache, out):
             v_grouped[b] = keep.tile(
                 [P, HK * D, 4], BF16, name="v_grouped%d" % b, align_bytes=64
             )
-            nc.vector.tensor_copy(
-                out=v_grouped[b][:], in_=v_rows[b][:].rearrange("p t c -> p c t")
+            nc.gpsimd.tensor_scalar(
+                out=v_grouped[b][:],
+                in0=v_rows[b][:].rearrange("p t c -> p c t"),
+                scalar1=1.0,
+                scalar2=0.0,
+                op0=ALU.mult,
+                op1=ALU.add,
             )
 
         def quantise_v(b):
@@ -308,9 +313,9 @@ def tile_radixattention_s_kernel(tc, q, k, v, k_cache, v_cache, out):
             when(unit(s + 2), exp_bias)
             when(pair_that_ends_at(s - 3), normalise_and_store)
 
-            when(pair_that_ends_at(s - 2), multiply_v)
             when(unit(s), exponentials)
             when(pair_that_ends_at(s), transpose_e)
+            when(pair_that_ends_at(s - 2), multiply_v)
             when(pair_that_ends_at(s - 1), regroup_e)
             when(sequence_that_starts_at(s + 5), copy_qk)
 

@@ -121,8 +121,8 @@ def tile_radixattention_s_kernel(tc, q, k, v, k_cache, v_cache, out):
             qT[b] = keep.tile([P, H * E], BF16, name="qT%d" % b)
             kT[b] = keep.tile([P, HK, S], BF16, name="kT%d" % b)
             nc.scalar.copy(out=qT[b][:], in_=qT_ps[b][:])
-            nc.vector.tensor_copy(out=kT[b][:, 0, :], in_=kT_ps[b, 0][:])
-            nc.scalar.copy(out=kT[b][:, 1, :], in_=kT_ps[b, 1][:])
+            for g in range(HK):
+                nc.scalar.copy(out=kT[b][:, g, :], in_=kT_ps[b, g][:])
 
         def regroup_v(b):
             v_grouped[b] = keep.tile(
@@ -148,6 +148,10 @@ def tile_radixattention_s_kernel(tc, q, k, v, k_cache, v_cache, out):
 
         def score_diag(b):
             diag_ps[b] = banks.tile([P, H, E], F32, name="diag_ps", tag="bank")
+            prefix_max[b] = keep.tile([P, H], F32, name="prefix_max%d" % b)
+            neg_max[b] = keep.tile([P, H], F32, name="neg_max%d" % b)
+            prefix_sum[b] = keep.tile([P, H], F32, name="prefix_sum%d" % b)
+            diag_sum[b] = keep.tile([P, H], F32, name="diag_sum%d" % b)
             for h in range(H):
                 nc.tensor.matmul(
                     out=diag_ps[b][:, h, :],
@@ -159,10 +163,6 @@ def tile_radixattention_s_kernel(tc, q, k, v, k_cache, v_cache, out):
 
         def mask_diag(b):
             masked[b] = keep.tile([P, H, E], F32, name="masked%d" % b)
-            prefix_max[b] = keep.tile([P, H], F32, name="prefix_max%d" % b)
-            neg_max[b] = keep.tile([P, H], F32, name="neg_max%d" % b)
-            prefix_sum[b] = keep.tile([P, H], F32, name="prefix_sum%d" % b)
-            diag_sum[b] = keep.tile([P, H], F32, name="diag_sum%d" % b)
             nc.vector.tensor_tensor(
                 out=masked[b][:],
                 in0=diag_ps[b][:],
@@ -222,29 +222,30 @@ def tile_radixattention_s_kernel(tc, q, k, v, k_cache, v_cache, out):
                 accum_out=diag_sum[b][:, h : h + 1],
             )
 
-        def transpose_e(p):
-            eT_ps[p] = banks.tile([P, G, 2, E], F32, name="eT_ps", tag="bank")
-            for a in range(G):
-                words = e_rows[p * G + a][:].bitcast(F32)
-                for u in range(2):
-                    nc.tensor.transpose(
-                        eT_ps[p][:, a, u, :], words[:, u * P : (u + 1) * P], ident_f32[:]
-                    )
+        def transpose_e(n):
+            eT_ps[n] = banks.tile([P, 2, E], F32, name="eT_ps", tag="bank")
+            words = e_rows[n][:].bitcast(F32)
+            for u in range(2):
+                nc.tensor.transpose(eT_ps[n][:, u, :], words[:, u * P : (u + 1) * P], ident_f32[:])
 
-        def regroup_e(p):
-            e_grouped[p] = keep.tile(
-                [P, G * E * 4], BF16, name="e_grouped%d" % p, align_bytes=64
-            )
+        def regroup_e(n):
+            p, a = divmod(n, G)
+            if a == 0:
+                e_grouped[p] = keep.tile(
+                    [P, G, E * 4], BF16, name="e_grouped%d" % p, align_bytes=64
+                )
             nc.scalar.copy(
-                out=e_grouped[p][:].bitcast(F32).rearrange("p (a i u) -> p a i u", a=G, u=2),
-                in_=eT_ps[p][:].rearrange("p a u i -> p a i u"),
+                out=e_grouped[p][:, a, :].bitcast(F32).rearrange("p (i u) -> p i u", u=2),
+                in_=eT_ps[n][:].rearrange("p u i -> p i u"),
             )
 
         def quantise_e(p):
             e_codes[p] = keep.tile([P, G * E], U32, name="e_codes%d" % p, align_bytes=64)
             e_scales[p] = keep.tile([P, G * E], U8, name="e_scales%d" % p, align_bytes=64)
             nc.vector.quantize_mx(
-                out=e_codes[p][:].bitcast(FP8X4), scales=e_scales[p][:], in_=e_grouped[p][:]
+                out=e_codes[p][:].bitcast(FP8X4),
+                scales=e_scales[p][:],
+                in_=e_grouped[p][:].rearrange("p a c -> p (a c)"),
             )
 
         def multiply_v(p):
@@ -302,23 +303,22 @@ def tile_radixattention_s_kernel(tc, q, k, v, k_cache, v_cache, out):
 
         for s in range(-5, N_HEADS + 3):
             when(sequence_that_starts_at(s + 5), transpose_qk)
-            when(sequence_that_starts_at(s + 4), score_diag)
             when(unit(s + 3), score_prefix)
+            when(sequence_that_starts_at(s + 3), score_diag)
 
             when(sequence_that_starts_at(s - 4), sum_rows)
             when(unit(s + 2), max_prefix)
+            when(sequence_that_starts_at(s + 2), mask_diag)
             when(pair_that_ends_at(s - 2), quantise_e)
-            when(sequence_that_starts_at(s + 2), max_diag)
             when(sequence_that_starts_at(s - 4), invert_sums)
-            when(unit(s + 2), exp_bias)
             when(pair_that_ends_at(s - 3), normalise_and_store)
+            when(sequence_that_starts_at(s + 2), max_diag)
+            when(unit(s + 2), exp_bias)
+            when(sequence_that_starts_at(s - 2), quantise_v)
 
             when(unit(s), exponentials)
-            when(pair_that_ends_at(s), transpose_e)
+            when(unit(s), transpose_e)
             when(pair_that_ends_at(s - 2), multiply_v)
-            when(pair_that_ends_at(s - 1), regroup_e)
+            when(unit(s - 1), regroup_e)
             when(sequence_that_starts_at(s + 5), copy_qk)
-
-            when(sequence_that_starts_at(s + 3), mask_diag)
             when(sequence_that_starts_at(s), regroup_v)
-            when(sequence_that_starts_at(s - 2), quantise_v)

@@ -273,10 +273,9 @@ def tile_radixattention_s_kernel(tc, q, k, v, k_cache, v_cache, out):
             inv_sum[b] = keep.tile([P, H], F32, name="inv_sum%d" % b)
             nc.vector.reciprocal(out=inv_sum[b][:], in_=row_sum[b][:])
 
-        def normalise_and_store(p):
-            b, g = divmod(p, HK)
+        def normalise_and_store(b, g):
             heads = slice(g * G, (g + 1) * G)
-            o_sb = keep.tile([P, G, D], F32, name="o_sb%d" % p)
+            o_sb = keep.tile([P, G, D], F32, name="o_sb%d_%d" % (b, g))
             nc.vector.tensor_tensor(
                 out=o_sb[:],
                 in0=o_ps[b][:, heads, :],
@@ -295,30 +294,33 @@ def tile_radixattention_s_kernel(tc, q, k, v, k_cache, v_cache, out):
         def unit(n):
             return n if 0 <= n < N_HEADS else None
 
-        load_qk(0)
         for b in range(B):
-            if b + 1 < B:
-                load_qk(b + 1)
+            load_qk(b)
             load_v(b)
+        for b in range(B):
+            regroup_v(b)
 
         for s in range(-5, N_HEADS + 3):
             when(sequence_that_starts_at(s + 5), transpose_qk)
             when(unit(s + 3), score_prefix)
             when(sequence_that_starts_at(s + 3), score_diag)
 
-            when(sequence_that_starts_at(s - 4), sum_rows)
+            finished = sequence_that_starts_at(s - 6)
             when(unit(s + 2), max_prefix)
             when(sequence_that_starts_at(s + 2), mask_diag)
+            when(sequence_that_starts_at(s - 5), sum_rows)
             when(pair_that_ends_at(s - 2), quantise_e)
-            when(sequence_that_starts_at(s - 4), invert_sums)
-            when(pair_that_ends_at(s - 3), normalise_and_store)
+            when(sequence_that_starts_at(s), quantise_v)
+            when(sequence_that_starts_at(s - 5), invert_sums)
+            if finished is not None:
+                normalise_and_store(finished, 0)
             when(sequence_that_starts_at(s + 2), max_diag)
+            if finished is not None:
+                normalise_and_store(finished, 1)
             when(unit(s + 2), exp_bias)
-            when(sequence_that_starts_at(s - 2), quantise_v)
 
             when(unit(s), exponentials)
             when(unit(s), transpose_e)
             when(pair_that_ends_at(s - 2), multiply_v)
             when(unit(s - 1), regroup_e)
             when(sequence_that_starts_at(s + 5), copy_qk)
-            when(sequence_that_starts_at(s), regroup_v)

@@ -300,27 +300,26 @@ def tile_radixattention_s_kernel(tc, q, k, v, k_cache, v_cache, out):
         for b in range(B):
             regroup_v(b)
 
-        for s in range(-5, N_HEADS + 3):
+        for s in range(-5, N_HEADS + 4):
             when(sequence_that_starts_at(s + 5), transpose_qk)
+            when(sequence_that_starts_at(s + 4), score_diag)
             when(unit(s + 3), score_prefix)
-            when(sequence_that_starts_at(s + 3), score_diag)
 
-            finished = sequence_that_starts_at(s - 6)
+            finished = sequence_that_starts_at(s - 7)
             when(unit(s + 2), max_prefix)
-            when(sequence_that_starts_at(s + 2), mask_diag)
+            when(sequence_that_starts_at(s + 1), quantise_v)
+            when(sequence_that_starts_at(s + 3), mask_diag)
+            when(sequence_that_starts_at(s + 2), max_diag)
+            when(pair_that_ends_at(s - 3), quantise_e)
             when(sequence_that_starts_at(s - 5), sum_rows)
-            when(pair_that_ends_at(s - 2), quantise_e)
-            when(sequence_that_starts_at(s), quantise_v)
-            when(sequence_that_starts_at(s - 5), invert_sums)
+            when(sequence_that_starts_at(s - 6), invert_sums)
             if finished is not None:
                 normalise_and_store(finished, 0)
-            when(sequence_that_starts_at(s + 2), max_diag)
-            if finished is not None:
                 normalise_and_store(finished, 1)
             when(unit(s + 2), exp_bias)
 
             when(unit(s), exponentials)
             when(unit(s), transpose_e)
-            when(pair_that_ends_at(s - 2), multiply_v)
+            when(pair_that_ends_at(s - 3), multiply_v)
             when(unit(s - 1), regroup_e)
             when(sequence_that_starts_at(s + 5), copy_qk)

@@ -124,13 +124,15 @@ def tile_radixattention_s_kernel(tc, q, k, v, k_cache, v_cache, out):
             for g in range(HK):
                 nc.scalar.copy(out=kT[b][:, g, :], in_=kT_ps[b, g][:])
 
-        def regroup_v(b):
-            v_grouped[b] = keep.tile(
-                [P, HK * D, 4], BF16, name="v_grouped%d" % b, align_bytes=64
-            )
+        def regroup_v(b, g):
+            if g == 0:
+                v_grouped[b] = keep.tile(
+                    [P, HK * D, 4], BF16, name="v_grouped%d" % b, align_bytes=64
+                )
+            cols = slice(g * D, (g + 1) * D)
             nc.gpsimd.tensor_scalar(
-                out=v_grouped[b][:],
-                in0=v_rows[b][:].rearrange("p t c -> p c t"),
+                out=v_grouped[b][:, cols, :],
+                in0=v_rows[b][:, :, cols].rearrange("p t c -> p c t"),
                 scalar1=1.0,
                 scalar2=0.0,
                 op0=ALU.mult,
@@ -193,7 +195,7 @@ def tile_radixattention_s_kernel(tc, q, k, v, k_cache, v_cache, out):
 
         def exp_bias(n):
             b, h = divmod(n, H)
-            nc.vector.tensor_scalar(
+            nc.gpsimd.tensor_scalar(
                 out=neg_max[b][:, h : h + 1],
                 in0=prefix_max[b][:, h : h + 1],
                 scalar1=diag_max[b][:, h : h + 1],
@@ -265,7 +267,7 @@ def tile_radixattention_s_kernel(tc, q, k, v, k_cache, v_cache, out):
 
         def sum_rows(b):
             row_sum[b] = keep.tile([P, H], F32, name="row_sum%d" % b)
-            nc.vector.tensor_tensor(
+            nc.gpsimd.tensor_tensor(
                 out=row_sum[b][:], in0=prefix_sum[b][:], in1=diag_sum[b][:], op=ALU.add
             )
 
@@ -297,8 +299,6 @@ def tile_radixattention_s_kernel(tc, q, k, v, k_cache, v_cache, out):
         for b in range(B):
             load_qk(b)
             load_v(b)
-        for b in range(B):
-            regroup_v(b)
 
         for s in range(-5, N_HEADS + 4):
             when(sequence_that_starts_at(s + 5), transpose_qk)
@@ -317,6 +317,8 @@ def tile_radixattention_s_kernel(tc, q, k, v, k_cache, v_cache, out):
                 normalise_and_store(finished, 0)
                 normalise_and_store(finished, 1)
             when(unit(s + 2), exp_bias)
+            when(sequence_that_starts_at(s + 5), lambda b: regroup_v(b, 0))
+            when(sequence_that_starts_at(s + 3), lambda b: regroup_v(b, 1))
 
             when(unit(s), exponentials)
             when(unit(s), transpose_e)

import math
from contextlib import ExitStack

import concourse.mybir as mybir
from concourse.masks import make_identity

BF16 = mybir.dt.bfloat16
F32 = mybir.dt.float32
U32 = mybir.dt.uint32
U8 = mybir.dt.uint8
FP8X4 = mybir.dt.float8_e4m3fn_x4
ALU = mybir.AluOpType
ACT = mybir.ActivationFunctionType
AX = mybir.AxisListType

B = 4
E = 128
PREFIX = 384
S = PREFIX + E
H = 4
HK = 2
G = H // HK
D = 128
P = 128
SCALING = 1.0 / math.sqrt(D)
HIDDEN = -1.0e30

FLOPS = 2 * 2 * B * H * E * S * D


N_HEADS = B * H
N_PAIRS = B * HK


def sequence_that_starts_at(n):
    return n // H if 0 <= n < N_HEADS and n % H == 0 else None


def pair_that_ends_at(n):
    return n // G if 0 <= n < N_HEADS and n % G == G - 1 else None


def tile_radixattention_s_kernel(tc, q, k, v, k_cache, v_cache, out):
    nc = tc.nc
    with ExitStack() as ctx:
        consts = ctx.enter_context(tc.tile_pool(name="consts", bufs=1))
        keep = ctx.enter_context(tc.tile_pool(name="keep", bufs=1))
        banks = ctx.enter_context(tc.psum_pool(name="banks", bufs=8))
        ctx.enter_context(tc.manual_schedule())

        ident_bf = consts.tile([P, P], BF16, name="ident_bf")
        make_identity(nc, ident_bf[:])
        causal = consts.tile([P, E], F32, name="causal")
        nc.gpsimd.memset(causal[:], 0.0)
        nc.gpsimd.affine_select(
            out=causal[:],
            in_=causal[:],
            compare_op=ALU.is_ge,
            fill=HIDDEN,
            base=0,
            pattern=[[-1, E]],
            channel_multiplier=1,
        )
        ident_f32 = consts.tile([P, P], F32, name="ident_f32")
        make_identity(nc, ident_f32[:])
        warm_in = consts.tile([P, 1], F32, name="warm_in")
        warm_out = consts.tile([P, 1], F32, name="warm_out")
        nc.vector.memset(warm_in[:], 0.0)
        nc.scalar.activation(out=warm_out[:], in_=warm_in[:], func=ACT.Exp)

        q_rows, k_rows, v_rows = {}, {}, {}
        qT_ps, kT_ps, qT, kT = {}, {}, {}, {}
        v_grouped, v_codes, v_scales = {}, {}, {}
        diag_ps, masked, diag_max, prefix_max, neg_max = {}, {}, {}, {}, {}
        prefix_sum, diag_sum, row_sum, inv_sum = {}, {}, {}, {}
        prefix_ps, e_rows = {}, {}
        eT_ps, e_grouped, e_codes, e_scales, o_ps = {}, {}, {}, {}, {}

        def load_qk(b):
            q_rows[b] = keep.tile([P, H * D], BF16, name="q_rows%d" % b)
            nc.sync.dma_start(out=q_rows[b][:], in_=q[b].rearrange("e h d -> e (h d)"))
            k_rows[b] = keep.tile([P, S // P, HK * D], BF16, name="k_rows%d" % b)
            nc.sync.dma_start(
                out=k_rows[b][:, 0 : PREFIX // P, :],
                in_=k_cache[b].rearrange("(t p) g d -> p t (g d)", p=P),
            )
            nc.sync.dma_start(
                out=k_rows[b][:, PREFIX // P, :], in_=k[b].rearrange("e g d -> e (g d)")
            )

        def load_v(b):
            v_rows[b] = keep.tile([P, 4, HK * D], BF16, name="v_rows%d" % b)
            nc.sync.dma_start(
                out=v_rows[b][:, 0:2, :].rearrange("p t c -> p (t c)"),
                in_=v_cache[b, 0:256].rearrange("(p e) g d -> p (e g d)", e=2),
            )
            nc.sync.dma_start(
                out=v_rows[b][0:64, 2:4, :].rearrange("p t c -> p (t c)"),
                in_=v_cache[b, 256:PREFIX].rearrange("(p e) g d -> p (e g d)", e=2),
            )
            nc.sync.dma_start(
                out=v_rows[b][64:P, 2:4, :].rearrange("p t c -> p (t c)"),
                in_=v[b].rearrange("(p e) g d -> p (e g d)", e=2),
            )

        def transpose_qk(b):
            qT_ps[b] = banks.tile([P, H * E], BF16, name="qT_ps", tag="bank")
            for h in range(H):
                cols = slice(h * D, (h + 1) * D)
                nc.tensor.transpose(qT_ps[b][:, cols], q_rows[b][:, cols], ident_bf[:])
            for g in range(HK):
                kT_ps[b, g] = banks.tile([P, S], BF16, name="kT_ps", tag="bank")
                for t in range(S // P):
                    nc.tensor.transpose(
                        kT_ps[b, g][:, t * P : (t + 1) * P],
                        k_rows[b][:, t, g * D : (g + 1) * D],
                        ident_bf[:],
                    )

        def copy_qk(b):
            qT[b] = keep.tile([P, H * E], BF16, name="qT%d" % b)
            kT[b] = keep.tile([P, HK, S], BF16, name="kT%d" % b)
            nc.scalar.copy(out=qT[b][:], in_=qT_ps[b][:])
            for g in range(HK):
                nc.scalar.copy(out=kT[b][:, g, :], in_=kT_ps[b, g][:])

        def regroup_v(b, g):
            if g == 0:
                v_grouped[b] = keep.tile(
                    [P, HK * D, 4], BF16, name="v_grouped%d" % b, align_bytes=64
                )
            cols = slice(g * D, (g + 1) * D)
            nc.gpsimd.tensor_scalar(
                out=v_grouped[b][:, cols, :],
                in0=v_rows[b][:, :, cols].rearrange("p t c -> p c t"),
                scalar1=1.0,
                scalar2=0.0,
                op0=ALU.mult,
                op1=ALU.add,
            )

        def quantise_v(b):
            v_codes[b] = keep.tile([P, HK * D], U32, name="v_codes%d" % b, align_bytes=64)
            v_scales[b] = keep.tile([P, HK * D], U8, name="v_scales%d" % b, align_bytes=64)
            nc.vector.quantize_mx(
                out=v_codes[b][:].bitcast(FP8X4),
                scales=v_scales[b][:],
                in_=v_grouped[b][:].rearrange("p c t -> p (c t)"),
            )

        def score_diag(b):
            diag_ps[b] = banks.tile([P, H, E], F32, name="diag_ps", tag="bank")
            prefix_max[b] = keep.tile([P, H], F32, name="prefix_max%d" % b)
            neg_max[b] = keep.tile([P, H], F32, name="neg_max%d" % b)
            prefix_sum[b] = keep.tile([P, H], F32, name="prefix_sum%d" % b)
            diag_sum[b] = keep.tile([P, H], F32, name="diag_sum%d" % b)
            for h in range(H):
                nc.tensor.matmul(
                    out=diag_ps[b][:, h, :],
                    lhsT=qT[b][:, h * E : (h + 1) * E],
                    rhs=kT[b][:, h // G, PREFIX:S],
                    start=True,
                    stop=True,
                )

        def mask_diag(b):
            masked[b] = keep.tile([P, H, E], F32, name="masked%d" % b)
            nc.vector.tensor_tensor(
                out=masked[b][:],
                in0=diag_ps[b][:],
                in1=causal[:].unsqueeze(1).to_broadcast([P, H, E]),
                op=ALU.add,
            )

        def max_diag(b):
            diag_max[b] = keep.tile([P, H], F32, name="diag_max%d" % b)
            nc.vector.tensor_reduce(out=diag_max[b][:], in_=masked[b][:], axis=AX.X, op=ALU.max)

        def score_prefix(n):
            b, h = divmod(n, H)
            prefix_ps[n] = banks.tile([P, PREFIX], F32, name="prefix_ps", tag="bank")
            nc.tensor.matmul(
                out=prefix_ps[n][:],
                lhsT=qT[b][:, h * E : (h + 1) * E],
                rhs=kT[b][:, h // G, 0:PREFIX],
                start=True,
                stop=True,
            )

        def max_prefix(n):
            b, h = divmod(n, H)
            nc.vector.tensor_reduce(
                out=prefix_max[b][:, h : h + 1], in_=prefix_ps[n][:], axis=AX.X, op=ALU.max
            )

        def exp_bias(n):
            b, h = divmod(n, H)
            nc.gpsimd.tensor_scalar(
                out=neg_max[b][:, h : h + 1],
                in0=prefix_max[b][:, h : h + 1],
                scalar1=diag_max[b][:, h : h + 1],
                scalar2=-SCALING,
                op0=ALU.max,
                op1=ALU.mult,
            )

        def exponentials(n):
            b, h = divmod(n, H)
            e_rows[n] = keep.tile([P, S], BF16, name="e_rows%d" % n)
            nc.scalar.activation(
                out=e_rows[n][:, 0:PREFIX],
                in_=prefix_ps[n][:],
                func=ACT.Exp,
                bias=neg_max[b][:, h : h + 1],
                scale=SCALING,
                accum_out=prefix_sum[b][:, h : h + 1],
            )
            nc.scalar.activation(
                out=e_rows[n][:, PREFIX:S],
                in_=masked[b][:, h, :],
                func=ACT.Exp,
                bias=neg_max[b][:, h : h + 1],
                scale=SCALING,
                accum_out=diag_sum[b][:, h : h + 1],
            )

        def transpose_e(n):
            eT_ps[n] = banks.tile([P, 2, E], F32, name="eT_ps", tag="bank")
            words = e_rows[n][:].bitcast(F32)
            for u in range(2):
                nc.tensor.transpose(eT_ps[n][:, u, :], words[:, u * P : (u + 1) * P], ident_f32[:])

        def regroup_e(n):
            p, a = divmod(n, G)
            if a == 0:
                e_grouped[p] = keep.tile(
                    [P, G, E * 4], BF16, name="e_grouped%d" % p, align_bytes=64
                )
            nc.scalar.copy(
                out=e_grouped[p][:, a, :].bitcast(F32).rearrange("p (i u) -> p i u", u=2),
                in_=eT_ps[n][:].rearrange("p u i -> p i u"),
            )

        def quantise_e(p):
            e_codes[p] = keep.tile([P, G * E], U32, name="e_codes%d" % p, align_bytes=64)
            e_scales[p] = keep.tile([P, G * E], U8, name="e_scales%d" % p, align_bytes=64)
            nc.vector.quantize_mx(
                out=e_codes[p][:].bitcast(FP8X4),
                scales=e_scales[p][:],
                in_=e_grouped[p][:].rearrange("p a c -> p (a c)"),
            )

        def multiply_v(p):
            b, g = divmod(p, HK)
            if g == 0:
                o_ps[b] = banks.tile([P, H, D], F32, name="o_ps", tag="bank")
            for a in range(G):
                nc.tensor.matmul_mx(
                    out=o_ps[b][:, g * G + a, :],
                    lhsT=e_codes[p][:, a * E : (a + 1) * E].bitcast(FP8X4),
                    lhsT_scale=e_scales[p][:, a * E : (a + 1) * E],
                    rhs=v_codes[b][:, g * D : (g + 1) * D].bitcast(FP8X4),
                    rhs_scale=v_scales[b][:, g * D : (g + 1) * D],
                    start=True,
                    stop=True,
                )

        def sum_rows(b):
            row_sum[b] = keep.tile([P, H], F32, name="row_sum%d" % b)
            nc.gpsimd.tensor_tensor(
                out=row_sum[b][:], in0=prefix_sum[b][:], in1=diag_sum[b][:], op=ALU.add
            )

        def invert_sums(b):
            inv_sum[b] = keep.tile([P, H], F32, name="inv_sum%d" % b)
            nc.vector.reciprocal(out=inv_sum[b][:], in_=row_sum[b][:])

        def normalise_and_store(b, g):
            heads = slice(g * G, (g + 1) * G)
            o_sb = keep.tile([P, G, D], F32, name="o_sb%d_%d" % (b, g))
            nc.vector.tensor_tensor(
                out=o_sb[:],
                in0=o_ps[b][:, heads, :],
                in1=inv_sum[b][:, heads].unsqueeze(2).to_broadcast([P, G, D]),
                op=ALU.mult,
            )
            nc.sync.dma_start(
                out=out[b * E : (b + 1) * E, g * G * D : (g + 1) * G * D],
                in_=o_sb[:].rearrange("p a d -> p (a d)"),
            )

        def when(index, stage):
            if index is not None:
                stage(index)

        def unit(n):
            return n if 0 <= n < N_HEADS else None

        for b in range(B):
            load_qk(b)
            load_v(b)

        for s in range(-5, N_HEADS + 4):
            when(sequence_that_starts_at(s + 5), transpose_qk)
            when(sequence_that_starts_at(s + 4), score_diag)
            when(unit(s + 3), score_prefix)

            finished = sequence_that_starts_at(s - 7)
            when(unit(s + 2), max_prefix)
            when(sequence_that_starts_at(s + 1), quantise_v)
            when(sequence_that_starts_at(s + 3), mask_diag)
            when(sequence_that_starts_at(s + 2), max_diag)
            when(pair_that_ends_at(s - 3), quantise_e)
            when(sequence_that_starts_at(s - 5), sum_rows)
            when(sequence_that_starts_at(s - 6), invert_sums)
            if finished is not None:
                normalise_and_store(finished, 0)
                normalise_and_store(finished, 1)
            when(unit(s + 2), exp_bias)
            when(sequence_that_starts_at(s + 5), lambda b: regroup_v(b, 0))
            when(sequence_that_starts_at(s + 3), lambda b: regroup_v(b, 1))

            when(unit(s), exponentials)
            when(unit(s), transpose_e)
            when(pair_that_ends_at(s - 3), multiply_v)
            when(unit(s - 1), regroup_e)
            when(sequence_that_starts_at(s + 5), copy_qk)
